import numpy as np
import ml_dtypes


def mxq(x, axis, fmt="e4m3"):
    dtype, down = {"e4m3": (ml_dtypes.float8_e4m3fn, 7), "e5m2": (ml_dtypes.float8_e5m2, 14)}[fmt]
    v = np.moveaxis(np.asarray(x, np.float32).astype(ml_dtypes.bfloat16).astype(np.float64), axis, -1)
    blocks = v.reshape(v.shape[:-1] + (-1, 32))
    amax = np.abs(blocks).max(-1, keepdims=True)
    byte = np.maximum(np.where(amax > 0, np.frexp(amax)[1] - 1 + 127, 0) - down, 1)
    scale = np.exp2(byte - 127.0)
    codes = (blocks / scale).astype(np.float32).astype(dtype).astype(np.float64)
    return np.moveaxis((codes * scale).reshape(v.shape), -1, axis)


WIDE = False


def mx_kscale(k):
    if not WIDE:
        return np.ones(k)
    levels = np.array([10, -10, 5, -5, 0])
    a = np.random.permutation(np.resize(levels, k // 512 * 4)).reshape(k // 512, 4)
    idx = np.arange(k)
    return np.exp2(a[idx // 512, idx % 128 // 32])


BF16 = ml_dtypes.bfloat16


def bf(x):
    return np.asarray(x, np.float32).astype(BF16)


def f64(x):
    return np.asarray(x).astype(np.float64)


E2M1 = np.array([0.0, 0.5, 1.0, 1.5, 2.0, 3.0, 4.0, 6.0, -0.0, -0.5, -1.0, -1.5, -2.0, -3.0, -4.0, -6.0])


def pack_weight(w, fmt):
    k, n = w.shape
    w = f64(bf(w)).reshape(k // 32, 32, n)
    amax = np.abs(w).max(1)
    if fmt == "e4m3":
        byte = np.frexp(amax)[1] - 1 + 127 - 7
    else:
        mant, ex = np.frexp(amax / 6.0)
        byte = np.where(mant > 0.5, ex, ex - 1) + 127
    byte = np.clip(np.where(amax > 0, byte, 1), 1, 254)
    scaled = (w * np.exp2(127.0 - byte)[:, None, :]).reshape(k, n).astype(np.float32)
    by_word = np.ascontiguousarray(scaled.reshape(k // 512, 128, 4, n).transpose(0, 1, 3, 2))
    if fmt == "e4m3":
        words = by_word.astype(ml_dtypes.float8_e4m3fn).view(np.uint8)
    else:
        c = by_word.astype(ml_dtypes.float4_e2m1fn).view(np.uint8) & 0xF
        words = c[..., 0::2] | (c[..., 1::2] << 4)
    return np.ascontiguousarray(words), np.ascontiguousarray(byte.astype(np.uint8).reshape(k // 512, 16, n))


def unpack_weight(words, scales, fmt):
    g, p, n, _ = words.shape
    if fmt == "e4m3":
        vals = np.ascontiguousarray(words).view(ml_dtypes.float8_e4m3fn).astype(np.float64)
    else:
        nib = np.empty((g, p, n, 4), np.uint8)
        nib[..., 0::2] = words & 0xF
        nib[..., 1::2] = words >> 4
        vals = E2M1[nib]
    vals = vals * np.repeat(np.exp2(scales.astype(np.float64) - 127.0), 8, axis=1)[..., None]
    return vals.transpose(0, 1, 3, 2).reshape(g * 512, n)


B, NP, H, W, EMB = 2, 128, 16, 32, 512
L = NP + H * W
C2 = EMB + EMB
BN_EPS = 1e-5


def setup_inputs():
    s = mx_kscale(C2)
    T1 = bf(np.random.standard_normal((B, L, EMB)) * s[:EMB])
    T2 = bf(np.random.standard_normal((B, L, EMB)) * s[EMB:])
    Wf = np.random.standard_normal((EMB, C2)) / np.sqrt(C2) / s[None, :]
    Wf_words, Wf_scales = pack_weight(np.ascontiguousarray(Wf.T), 'e4m3')
    bn_g = bf(1.0 + 0.1 * np.random.standard_normal(EMB))
    bn_b = bf(0.3 * np.random.standard_normal(EMB))
    return {'T1': T1,
            'T2': T2,
            'Wf_words': Wf_words,
            'Wf_scales': Wf_scales,
            'bn_g': bn_g,
            'bn_b': bn_b}


def reference(T1, T2, Wf_words, Wf_scales, bn_g, bn_b):
    joint = np.concatenate([f64(T1).swapaxes(1, 2), f64(T2).swapaxes(1, 2)], axis=1)
    y = unpack_weight(Wf_words, Wf_scales, 'e4m3').T @ mxq(joint, 1, 'e4m3')
    mu = y.mean(axis=(0, 2), keepdims=True)
    var = y.var(axis=(0, 2), keepdims=True)
    y = (y - mu) / np.sqrt(var + BN_EPS)
    y = y * f64(bn_g)[None, :, None] + f64(bn_b)[None, :, None]
    y = np.maximum(y, 0.0)
    return y.swapaxes(1, 2)

@@ -1,0 +1,198 @@
+from contextlib import ExitStack
+
+import concourse.mybir as mybir
+from concourse.masks import make_identity
+
+F32 = mybir.dt.float32
+BF16 = mybir.dt.bfloat16
+I32 = mybir.dt.int32
+U32 = mybir.dt.uint32
+U8 = mybir.dt.uint8
+FP8X4 = mybir.dt.float8_e4m3fn_x4
+ACT = mybir.ActivationFunctionType
+
+P = 128
+ROWS = 1280
+EMB = 512
+STREAMS = 2
+ROW_TILES = ROWS // P
+TILES_PER_CHUNK = 2
+CHUNKS = ROW_TILES // TILES_PER_CHUNK
+CHUNK_ROWS = TILES_PER_CHUNK * P
+O_TILES = EMB // P
+HALVES = 2
+O_PER_HALF = O_TILES // HALVES
+WORDS = EMB // 2
+BN_EPS = 1e-5
+BN_STATS_DIM = 6
+
+FLOPS = 2 * ROWS * STREAMS * EMB * EMB
+
+
+def tile_iag_pb_kernel(tc, T1, T2, Wf_words, Wf_scales, bn_g, bn_b, out):
+    nc = tc.nc
+    streams = [t.flatten_outer_dims().rearrange("(p i) c -> p i c", i=ROW_TILES) for t in (T1, T2)]
+    out_rows = out.flatten_outer_dims().rearrange("(p i) o -> p i o", i=ROW_TILES)
+
+    with ExitStack() as ctx:
+        keep = ctx.enter_context(tc.tile_pool(name="keep", bufs=1))
+        stage = ctx.enter_context(tc.tile_pool(name="stage", bufs=3))
+        norm_pool = ctx.enter_context(tc.tile_pool(name="norm", bufs=CHUNKS))
+        psum_y = ctx.enter_context(tc.psum_pool(name="psum_y", bufs=6))
+        psum_tr = ctx.enter_context(tc.psum_pool(name="psum_tr", bufs=2))
+
+        gb_rows = keep.tile([2 * O_TILES, P], BF16, name="gb_rows")
+        nc.scalar.dma_start(out=gb_rows[0:O_TILES, :], in_=bn_g.rearrange("(j o) -> j o", o=P))
+        nc.scalar.dma_start(out=gb_rows[O_TILES : 2 * O_TILES, :], in_=bn_b.rearrange("(j o) -> j o", o=P))
+
+        eps = keep.tile([P, 1], F32, name="eps")
+        nc.vector.memset(eps[:], BN_EPS)
+        warm = keep.tile([P, 1], F32, name="warm")
+        nc.scalar.activation(out=warm[:], in_=eps[:], func=ACT.Sqrt)
+
+        w_scales = keep.tile([P, STREAMS, EMB], U8, name="w_scales", align_bytes=64)
+        nc.vector.memset(w_scales[:].rearrange("p g n -> p (g n)").bitcast(I32), 0)
+        gb_wide = keep.tile([P, P], F32, name="gb_wide")
+        nc.vector.memset(gb_wide[:], 0.0)
+
+        ident = keep.tile([P, P], F32, name="ident")
+        make_identity(nc, ident[:])
+
+        x_chunks = []
+
+        def load_chunk(c):
+            x_c = keep.tile([P, STREAMS, TILES_PER_CHUNK, EMB], BF16, name="x%d" % c)
+            for g in range(STREAMS):
+                nc.sync.dma_start(
+                    out=x_c[:, g, :, :],
+                    in_=streams[g][:, c * TILES_PER_CHUNK : (c + 1) * TILES_PER_CHUNK, :],
+                )
+            x_chunks.append(x_c)
+
+        load_chunk(0)
+        for r in range(4):
+            nc.sync.dma_start(
+                out=w_scales[r:P:32, :, :].bitcast(I32),
+                in_=Wf_scales[:, r:16:4, :].rearrange("g q n -> q g n").bitcast(I32),
+            )
+        w_words = keep.tile([P, STREAMS, EMB], U32, name="w_words", align_bytes=64)
+        for g in range(STREAMS):
+            nc.sync.dma_start(
+                out=w_words[:, g, :].bitcast(I32),
+                in_=Wf_words[g].rearrange("p n t -> p (n t)").bitcast(I32),
+            )
+        for c in range(1, CHUNKS):
+            load_chunk(c)
+
+        nc.vector.tensor_copy(out=gb_wide[0 : 2 * O_TILES, :], in_=gb_rows[:])
+        gb_t = psum_tr.tile([P, STREAMS, CHUNK_ROWS], F32, tag="tr")
+        nc.tensor.transpose(gb_t[:, 0, 0:P], gb_wide[:], ident[:])
+        gb_cols = keep.tile([P, 2 * O_TILES], F32, name="gb_cols")
+        nc.vector.tensor_copy(out=gb_cols[:], in_=gb_t[:, 0, 0 : 2 * O_TILES])
+        gain = gb_cols[:, 0:O_TILES]
+        offset = gb_cols[:, O_TILES : 2 * O_TILES]
+
+        stats = keep.tile([P, O_TILES, CHUNKS, BN_STATS_DIM], F32, name="stats")
+        mean_var = keep.tile([P, O_TILES, 2], F32, name="mean_var")
+        std = keep.tile([P, O_TILES], F32, name="std")
+        rstd = keep.tile([P, O_TILES], F32, name="rstd")
+        scale = keep.tile([P, O_TILES], F32, name="scale")
+        mean_scaled = keep.tile([P, O_TILES], F32, name="mean_scaled")
+        shift = keep.tile([P, O_TILES], F32, name="shift")
+
+        x_codes = []
+        x_scales = []
+
+        def transpose_and_quantise(c):
+            codes = keep.tile([P, STREAMS, CHUNK_ROWS], U32, name="x_codes%d" % c, align_bytes=64)
+            planes = keep.tile([P, STREAMS, CHUNK_ROWS], U8, name="x_scales%d" % c, align_bytes=64)
+            for g in range(STREAMS):
+                x_t = psum_tr.tile([P, 2, CHUNK_ROWS], F32, tag="tr")
+                for i in range(TILES_PER_CHUNK):
+                    words = x_chunks[c][:, g, i, :].bitcast(F32)
+                    for u in range(2):
+                        nc.tensor.transpose(x_t[:, u, i * P : (i + 1) * P], words[:, u:WORDS:2], ident[:])
+                grouped = stage.tile([P, CHUNK_ROWS, 4], BF16, tag="grouped", align_bytes=64)
+                nc.scalar.copy(out=grouped[:].bitcast(F32), in_=x_t[:].rearrange("p u r -> p r u"))
+                nc.vector.quantize_mx(
+                    out=codes[:, g, :].bitcast(FP8X4),
+                    scales=planes[:, g, :],
+                    in_=grouped[:].rearrange("p r t -> p (r t)"),
+                )
+            x_codes.append(codes)
+            x_scales.append(planes)
+
+        def multiply(h, c):
+            y = psum_y.tile([P, O_PER_HALF, CHUNK_ROWS], F32, tag="y")
+            for jj in range(O_PER_HALF):
+                j = h * O_PER_HALF + jj
+                for g in range(STREAMS):
+                    nc.tensor.matmul_mx(
+                        out=y[:, jj, :],
+                        lhsT=w_words[:, g, j * P : (j + 1) * P].bitcast(FP8X4),
+                        lhsT_scale=w_scales[:, g, j * P : (j + 1) * P],
+                        rhs=x_codes[c][:, g, :].bitcast(FP8X4),
+                        rhs_scale=x_scales[c][:, g, :],
+                        start=(g == 0),
+                        stop=(g == STREAMS - 1),
+                    )
+            for jj in range(O_PER_HALF):
+                nc.vector.bn_stats(out=stats[:, h * O_PER_HALF + jj, c, :], in_=y[:, jj, :])
+            return y
+
+        def scale_and_shift(h):
+            js = slice(h * O_PER_HALF, (h + 1) * O_PER_HALF)
+            for j in range(h * O_PER_HALF, (h + 1) * O_PER_HALF):
+                nc.vector.bn_aggr(out=mean_var[:, j, :], in_=stats[:, j, :, :].rearrange("p c s -> p (c s)"))
+            nc.scalar.activation(out=std[:, js], in_=mean_var[:, js, 1], func=ACT.Sqrt, bias=eps[:, 0:1])
+            nc.vector.reciprocal(out=rstd[:, js], in_=std[:, js])
+            nc.vector.tensor_mul(out=scale[:, js], in0=rstd[:, js], in1=gain[:, js])
+            nc.vector.tensor_mul(out=mean_scaled[:, js], in0=mean_var[:, js, 0], in1=scale[:, js])
+            nc.vector.tensor_sub(out=shift[:, js], in0=offset[:, js], in1=mean_scaled[:, js])
+
+        def normalise(h, y):
+            z = norm_pool.tile([P, O_PER_HALF, CHUNK_ROWS], F32, tag="z")
+            for jj in range(O_PER_HALF):
+                j = h * O_PER_HALF + jj
+                nc.scalar.activation(
+                    out=z[:, jj, :], in_=y[:, jj, :], func=ACT.Relu,
+                    bias=shift[:, j : j + 1], scale=scale[:, j : j + 1],
+                )
+            return z
+
+        def transpose_back_and_store(h, c, z, copy):
+            z_t = psum_tr.tile([P, TILES_PER_CHUNK, O_PER_HALF * P], F32, tag="tr")
+            for i in range(TILES_PER_CHUNK):
+                for jj in range(O_PER_HALF):
+                    nc.tensor.transpose(z_t[:, i, jj * P : (jj + 1) * P], z[:, jj, i * P : (i + 1) * P], ident[:])
+            result = stage.tile([P, TILES_PER_CHUNK, O_PER_HALF * P], F32, tag="result")
+            copy(out=result[:], in_=z_t[:])
+            nc.sync.dma_start(
+                out=out_rows[
+                    :,
+                    c * TILES_PER_CHUNK : (c + 1) * TILES_PER_CHUNK,
+                    h * O_PER_HALF * P : (h + 1) * O_PER_HALF * P,
+                ],
+                in_=result[:],
+            )
+
+        y_first = []
+        transpose_and_quantise(0)
+        for c in range(1, CHUNKS):
+            transpose_and_quantise(c)
+            y_first.append(multiply(0, c - 1))
+        y_first.append(multiply(0, CHUNKS - 1))
+        y_second = [multiply(1, 0)]
+        scale_and_shift(0)
+
+        z_first = []
+        for c in range(CHUNKS):
+            z_first.append(normalise(0, y_first[c]))
+            if c + 1 < CHUNKS:
+                y_second.append(multiply(1, c + 1))
+        scale_and_shift(1)
+        for c in range(CHUNKS):
+            transpose_back_and_store(0, c, z_first[c], nc.scalar.copy)
+        for c in range(CHUNKS):
+            z = normalise(1, y_second[c])
+            transpose_back_and_store(1, c, z, nc.vector.tensor_copy)

@@ -25,6 +25,8 @@ O_PER_HALF = O_TILES // HALVES
 WORDS = EMB // 2
 BN_EPS = 1e-5
 BN_STATS_DIM = 6
+HALF = O_PER_HALF * P
+SCALAR_COPIES = 2
 
 FLOPS = 2 * ROWS * STREAMS * EMB * EMB
 
@@ -36,22 +38,23 @@ def tile_iag_pb_kernel(tc, T1, T2, Wf_words, Wf_scales, bn_g, bn_b, out):
 
     with ExitStack() as ctx:
         keep = ctx.enter_context(tc.tile_pool(name="keep", bufs=1))
-        stage = ctx.enter_context(tc.tile_pool(name="stage", bufs=3))
+        stage = ctx.enter_context(tc.tile_pool(name="stage", bufs=4))
         norm_pool = ctx.enter_context(tc.tile_pool(name="norm", bufs=CHUNKS))
+        result_pool = ctx.enter_context(tc.tile_pool(name="result", bufs=HALVES * CHUNKS))
         psum_y = ctx.enter_context(tc.psum_pool(name="psum_y", bufs=6))
         psum_tr = ctx.enter_context(tc.psum_pool(name="psum_tr", bufs=2))
+        ctx.enter_context(tc.manual_schedule())
 
         gb_rows = keep.tile([2 * O_TILES, P], BF16, name="gb_rows")
         nc.scalar.dma_start(out=gb_rows[0:O_TILES, :], in_=bn_g.rearrange("(j o) -> j o", o=P))
         nc.scalar.dma_start(out=gb_rows[O_TILES : 2 * O_TILES, :], in_=bn_b.rearrange("(j o) -> j o", o=P))
 
+        w_scales = keep.tile([P, STREAMS, EMB], U8, name="w_scales", align_bytes=64)
+        nc.vector.memset(w_scales[:].rearrange("p g n -> p (g n)").bitcast(I32), 0)
         eps = keep.tile([P, 1], F32, name="eps")
         nc.vector.memset(eps[:], BN_EPS)
         warm = keep.tile([P, 1], F32, name="warm")
         nc.scalar.activation(out=warm[:], in_=eps[:], func=ACT.Sqrt)
-
-        w_scales = keep.tile([P, STREAMS, EMB], U8, name="w_scales", align_bytes=64)
-        nc.vector.memset(w_scales[:].rearrange("p g n -> p (g n)").bitcast(I32), 0)
         gb_wide = keep.tile([P, P], F32, name="gb_wide")
         nc.vector.memset(gb_wide[:], 0.0)
 
@@ -69,29 +72,28 @@ def tile_iag_pb_kernel(tc, T1, T2, Wf_words, Wf_scales, bn_g, bn_b, out):
                 )
             x_chunks.append(x_c)
 
+        w_words = keep.tile([P, STREAMS, EMB], U32, name="w_words", align_bytes=64)
+
+        def load_weight_half(h):
+            nc.sync.dma_start(
+                out=w_words[:, :, h * HALF : (h + 1) * HALF].bitcast(I32),
+                in_=Wf_words[:, :, h * HALF : (h + 1) * HALF, :].rearrange("g p n t -> p g (n t)").bitcast(I32),
+            )
+
         load_chunk(0)
         for r in range(4):
             nc.sync.dma_start(
                 out=w_scales[r:P:32, :, :].bitcast(I32),
                 in_=Wf_scales[:, r:16:4, :].rearrange("g q n -> q g n").bitcast(I32),
             )
-        w_words = keep.tile([P, STREAMS, EMB], U32, name="w_words", align_bytes=64)
-        for g in range(STREAMS):
-            nc.sync.dma_start(
-                out=w_words[:, g, :].bitcast(I32),
-                in_=Wf_words[g].rearrange("p n t -> p (n t)").bitcast(I32),
-            )
+        load_weight_half(0)
         for c in range(1, CHUNKS):
             load_chunk(c)
+        load_weight_half(1)
 
-        nc.vector.tensor_copy(out=gb_wide[0 : 2 * O_TILES, :], in_=gb_rows[:])
-        gb_t = psum_tr.tile([P, STREAMS, CHUNK_ROWS], F32, tag="tr")
-        nc.tensor.transpose(gb_t[:, 0, 0:P], gb_wide[:], ident[:])
         gb_cols = keep.tile([P, 2 * O_TILES], F32, name="gb_cols")
-        nc.vector.tensor_copy(out=gb_cols[:], in_=gb_t[:, 0, 0 : 2 * O_TILES])
         gain = gb_cols[:, 0:O_TILES]
         offset = gb_cols[:, O_TILES : 2 * O_TILES]
-
         stats = keep.tile([P, O_TILES, CHUNKS, BN_STATS_DIM], F32, name="stats")
         mean_var = keep.tile([P, O_TILES, 2], F32, name="mean_var")
         std = keep.tile([P, O_TILES], F32, name="std")
@@ -100,27 +102,35 @@ def tile_iag_pb_kernel(tc, T1, T2, Wf_words, Wf_scales, bn_g, bn_b, out):
         mean_scaled = keep.tile([P, O_TILES], F32, name="mean_scaled")
         shift = keep.tile([P, O_TILES], F32, name="shift")
 
-        x_codes = []
-        x_scales = []
+        def spread_gain_and_offset():
+            nc.vector.tensor_copy(out=gb_wide[0 : 2 * O_TILES, :], in_=gb_rows[:])
+            gb_t = psum_tr.tile([P, 2, CHUNK_ROWS], F32, tag="tr")
+            nc.tensor.transpose(gb_t[:, 0, 0:P], gb_wide[:], ident[:])
+            nc.vector.tensor_copy(out=gb_cols[:], in_=gb_t[:, 0, 0 : 2 * O_TILES])
 
-        def transpose_and_quantise(c):
-            codes = keep.tile([P, STREAMS, CHUNK_ROWS], U32, name="x_codes%d" % c, align_bytes=64)
-            planes = keep.tile([P, STREAMS, CHUNK_ROWS], U8, name="x_scales%d" % c, align_bytes=64)
-            for g in range(STREAMS):
-                x_t = psum_tr.tile([P, 2, CHUNK_ROWS], F32, tag="tr")
-                for i in range(TILES_PER_CHUNK):
-                    words = x_chunks[c][:, g, i, :].bitcast(F32)
-                    for u in range(2):
-                        nc.tensor.transpose(x_t[:, u, i * P : (i + 1) * P], words[:, u:WORDS:2], ident[:])
-                grouped = stage.tile([P, CHUNK_ROWS, 4], BF16, tag="grouped", align_bytes=64)
-                nc.scalar.copy(out=grouped[:].bitcast(F32), in_=x_t[:].rearrange("p u r -> p r u"))
-                nc.vector.quantize_mx(
-                    out=codes[:, g, :].bitcast(FP8X4),
-                    scales=planes[:, g, :],
-                    in_=grouped[:].rearrange("p r t -> p (r t)"),
-                )
-            x_codes.append(codes)
-            x_scales.append(planes)
+        x_codes = [
+            keep.tile([P, STREAMS, CHUNK_ROWS], U32, name="x_codes%d" % c, align_bytes=64) for c in range(CHUNKS)
+        ]
+        x_scales = [
+            keep.tile([P, STREAMS, CHUNK_ROWS], U8, name="x_scales%d" % c, align_bytes=64) for c in range(CHUNKS)
+        ]
+
+        def transpose_in(c, g):
+            x_t = psum_tr.tile([P, 2, CHUNK_ROWS], F32, tag="tr")
+            for i in range(TILES_PER_CHUNK):
+                words = x_chunks[c][:, g, i, :].bitcast(F32)
+                for u in range(2):
+                    nc.tensor.transpose(x_t[:, u, i * P : (i + 1) * P], words[:, u:WORDS:2], ident[:])
+            grouped = stage.tile([P, CHUNK_ROWS, 4], BF16, tag="grouped", align_bytes=64)
+            nc.scalar.copy(out=grouped[:].bitcast(F32), in_=x_t[:].rearrange("p u r -> p r u"))
+            return grouped
+
+        def quantise(c, g, grouped):
+            nc.vector.quantize_mx(
+                out=x_codes[c][:, g, :].bitcast(FP8X4),
+                scales=x_scales[c][:, g, :],
+                in_=grouped[:].rearrange("p r t -> p (r t)"),
+            )
 
         def multiply(h, c):
             y = psum_y.tile([P, O_PER_HALF, CHUNK_ROWS], F32, tag="y")
@@ -161,38 +171,40 @@ def tile_iag_pb_kernel(tc, T1, T2, Wf_words, Wf_scales, bn_g, bn_b, out):
             return z
 
         def transpose_back_and_store(h, c, z, copy):
-            z_t = psum_tr.tile([P, TILES_PER_CHUNK, O_PER_HALF * P], F32, tag="tr")
+            z_t = psum_tr.tile([P, TILES_PER_CHUNK, HALF], F32, tag="tr")
             for i in range(TILES_PER_CHUNK):
                 for jj in range(O_PER_HALF):
                     nc.tensor.transpose(z_t[:, i, jj * P : (jj + 1) * P], z[:, jj, i * P : (i + 1) * P], ident[:])
-            result = stage.tile([P, TILES_PER_CHUNK, O_PER_HALF * P], F32, tag="result")
+            result = result_pool.tile([P, TILES_PER_CHUNK, HALF], F32, tag="result")
             copy(out=result[:], in_=z_t[:])
             nc.sync.dma_start(
-                out=out_rows[
-                    :,
-                    c * TILES_PER_CHUNK : (c + 1) * TILES_PER_CHUNK,
-                    h * O_PER_HALF * P : (h + 1) * O_PER_HALF * P,
-                ],
+                out=out_rows[:, c * TILES_PER_CHUNK : (c + 1) * TILES_PER_CHUNK, h * HALF : (h + 1) * HALF],
                 in_=result[:],
             )
 
         y_first = []
-        transpose_and_quantise(0)
-        for c in range(1, CHUNKS):
-            transpose_and_quantise(c)
-            y_first.append(multiply(0, c - 1))
+        for c in range(CHUNKS):
+            grouped = [transpose_in(c, g) for g in range(STREAMS)]
+            if c == 1:
+                spread_gain_and_offset()
+            for g in range(STREAMS):
+                quantise(c, g, grouped[g])
+            if c >= 1:
+                y_first.append(multiply(0, c - 1))
         y_first.append(multiply(0, CHUNKS - 1))
-        y_second = [multiply(1, 0)]
         scale_and_shift(0)
+        y_second = [multiply(1, 0)]
 
         z_first = []
         for c in range(CHUNKS):
             z_first.append(normalise(0, y_first[c]))
             if c + 1 < CHUNKS:
                 y_second.append(multiply(1, c + 1))
-        scale_and_shift(1)
         for c in range(CHUNKS):
-            transpose_back_and_store(0, c, z_first[c], nc.scalar.copy)
+            copy = nc.scalar.copy if c < SCALAR_COPIES else nc.vector.tensor_copy
+            transpose_back_and_store(0, c, z_first[c], copy)
+            if c == 0:
+                scale_and_shift(1)
         for c in range(CHUNKS):
             z = normalise(1, y_second[c])
             transpose_back_and_store(1, c, z, nc.vector.tensor_copy)

@@ -25,6 +25,7 @@ O_PER_HALF = O_TILES // HALVES
 WORDS = EMB // 2
 BN_EPS = 1e-5
 BN_STATS_DIM = 6
+BANKS = 8
 HALF = O_PER_HALF * P
 SCALAR_COPIES = 2
 
@@ -41,9 +42,14 @@ def tile_iag_pb_kernel(tc, T1, T2, Wf_words, Wf_scales, bn_g, bn_b, out):
         stage = ctx.enter_context(tc.tile_pool(name="stage", bufs=4))
         norm_pool = ctx.enter_context(tc.tile_pool(name="norm", bufs=CHUNKS))
         result_pool = ctx.enter_context(tc.tile_pool(name="result", bufs=HALVES * CHUNKS))
-        psum_y = ctx.enter_context(tc.psum_pool(name="psum_y", bufs=6))
-        psum_tr = ctx.enter_context(tc.psum_pool(name="psum_tr", bufs=2))
+        psum = ctx.enter_context(tc.psum_pool(name="psum", bufs=1))
         ctx.enter_context(tc.manual_schedule())
+
+        def bank(k):
+            return psum.tile([P, 2, CHUNK_ROWS], F32, tag="bank%d" % k, name="bank%d" % k)
+
+        def y_bank(h, c):
+            return (h * CHUNKS + c) % BANKS
 
         gb_rows = keep.tile([2 * O_TILES, P], BF16, name="gb_rows")
         nc.scalar.dma_start(out=gb_rows[0:O_TILES, :], in_=bn_g.rearrange("(j o) -> j o", o=P))
@@ -104,7 +110,7 @@ def tile_iag_pb_kernel(tc, T1, T2, Wf_words, Wf_scales, bn_g, bn_b, out):
 
         def spread_gain_and_offset():
             nc.vector.tensor_copy(out=gb_wide[0 : 2 * O_TILES, :], in_=gb_rows[:])
-            gb_t = psum_tr.tile([P, 2, CHUNK_ROWS], F32, tag="tr")
+            gb_t = bank(CHUNKS - 1)
             nc.tensor.transpose(gb_t[:, 0, 0:P], gb_wide[:], ident[:])
             nc.vector.tensor_copy(out=gb_cols[:], in_=gb_t[:, 0, 0 : 2 * O_TILES])
 
@@ -116,7 +122,7 @@ def tile_iag_pb_kernel(tc, T1, T2, Wf_words, Wf_scales, bn_g, bn_b, out):
         ]
 
         def transpose_in(c, g):
-            x_t = psum_tr.tile([P, 2, CHUNK_ROWS], F32, tag="tr")
+            x_t = bank(CHUNKS + (c * STREAMS + g) % (BANKS - CHUNKS))
             for i in range(TILES_PER_CHUNK):
                 words = x_chunks[c][:, g, i, :].bitcast(F32)
                 for u in range(2):
@@ -133,7 +139,7 @@ def tile_iag_pb_kernel(tc, T1, T2, Wf_words, Wf_scales, bn_g, bn_b, out):
             )
 
         def multiply(h, c):
-            y = psum_y.tile([P, O_PER_HALF, CHUNK_ROWS], F32, tag="y")
+            y = bank(y_bank(h, c))
             for jj in range(O_PER_HALF):
                 j = h * O_PER_HALF + jj
                 for g in range(STREAMS):
@@ -146,15 +152,20 @@ def tile_iag_pb_kernel(tc, T1, T2, Wf_words, Wf_scales, bn_g, bn_b, out):
                         start=(g == 0),
                         stop=(g == STREAMS - 1),
                     )
-            for jj in range(O_PER_HALF):
-                nc.vector.bn_stats(out=stats[:, h * O_PER_HALF + jj, c, :], in_=y[:, jj, :])
             return y
 
-        def scale_and_shift(h):
+        def statistics(h, c, y):
+            for jj in range(O_PER_HALF):
+                nc.vector.bn_stats(out=stats[:, h * O_PER_HALF + jj, c, :], in_=y[:, jj, :])
+
+        def deviation(h):
             js = slice(h * O_PER_HALF, (h + 1) * O_PER_HALF)
             for j in range(h * O_PER_HALF, (h + 1) * O_PER_HALF):
                 nc.vector.bn_aggr(out=mean_var[:, j, :], in_=stats[:, j, :, :].rearrange("p c s -> p (c s)"))
             nc.scalar.activation(out=std[:, js], in_=mean_var[:, js, 1], func=ACT.Sqrt, bias=eps[:, 0:1])
+
+        def scale_and_shift(h):
+            js = slice(h * O_PER_HALF, (h + 1) * O_PER_HALF)
             nc.vector.reciprocal(out=rstd[:, js], in_=std[:, js])
             nc.vector.tensor_mul(out=scale[:, js], in0=rstd[:, js], in1=gain[:, js])
             nc.vector.tensor_mul(out=mean_scaled[:, js], in0=mean_var[:, js, 0], in1=scale[:, js])
@@ -170,8 +181,8 @@ def tile_iag_pb_kernel(tc, T1, T2, Wf_words, Wf_scales, bn_g, bn_b, out):
                 )
             return z
 
-        def transpose_back_and_store(h, c, z, copy):
-            z_t = psum_tr.tile([P, TILES_PER_CHUNK, HALF], F32, tag="tr")
+        def transpose_back_and_store(h, c, z, k, copy):
+            z_t = bank(k)
             for i in range(TILES_PER_CHUNK):
                 for jj in range(O_PER_HALF):
                     nc.tensor.transpose(z_t[:, i, jj * P : (jj + 1) * P], z[:, jj, i * P : (i + 1) * P], ident[:])
@@ -191,20 +202,30 @@ def tile_iag_pb_kernel(tc, T1, T2, Wf_words, Wf_scales, bn_g, bn_b, out):
                 quantise(c, g, grouped[g])
             if c >= 1:
                 y_first.append(multiply(0, c - 1))
+                statistics(0, c - 1, y_first[c - 1])
         y_first.append(multiply(0, CHUNKS - 1))
+        statistics(0, CHUNKS - 1, y_first[CHUNKS - 1])
+
+        deviation(0)
+        y_second = [multiply(1, c) for c in range(BANKS - CHUNKS)]
+        statistics(1, 0, y_second[0])
         scale_and_shift(0)
-        y_second = [multiply(1, 0)]
+        for c in range(1, BANKS - CHUNKS):
+            statistics(1, c, y_second[c])
 
         z_first = []
         for c in range(CHUNKS):
             z_first.append(normalise(0, y_first[c]))
-            if c + 1 < CHUNKS:
-                y_second.append(multiply(1, c + 1))
+            c_next = BANKS - CHUNKS + c
+            if c_next < CHUNKS:
+                y_second.append(multiply(1, c_next))
+                statistics(1, c_next, y_second[c_next])
         for c in range(CHUNKS):
             copy = nc.scalar.copy if c < SCALAR_COPIES else nc.vector.tensor_copy
-            transpose_back_and_store(0, c, z_first[c], copy)
+            transpose_back_and_store(0, c, z_first[c], 2 * CHUNKS - BANKS + c % (BANKS - CHUNKS), copy)
             if c == 0:
+                deviation(1)
                 scale_and_shift(1)
         for c in range(CHUNKS):
             z = normalise(1, y_second[c])
-            transpose_back_and_store(1, c, z, nc.vector.tensor_copy)
+            transpose_back_and_store(1, c, z, y_bank(1, c), nc.vector.tensor_copy)

@@ -27,7 +27,7 @@ BN_EPS = 1e-5
 BN_STATS_DIM = 6
 BANKS = 8
 HALF = O_PER_HALF * P
-SCALAR_COPIES = 2
+LAG = 2
 
 FLOPS = 2 * ROWS * STREAMS * EMB * EMB
 
@@ -60,7 +60,7 @@ def tile_iag_pb_kernel(tc, T1, T2, Wf_words, Wf_scales, bn_g, bn_b, out):
         eps = keep.tile([P, 1], F32, name="eps")
         nc.vector.memset(eps[:], BN_EPS)
         warm = keep.tile([P, 1], F32, name="warm")
-        nc.scalar.activation(out=warm[:], in_=eps[:], func=ACT.Sqrt)
+        nc.scalar.activation(out=warm[:], in_=eps[:], func=ACT.Abs_reciprocal_sqrt)
         gb_wide = keep.tile([P, P], F32, name="gb_wide")
         nc.vector.memset(gb_wide[:], 0.0)
 
@@ -87,13 +87,14 @@ def tile_iag_pb_kernel(tc, T1, T2, Wf_words, Wf_scales, bn_g, bn_b, out):
             )
 
         load_chunk(0)
+        load_chunk(1)
         for r in range(4):
             nc.sync.dma_start(
                 out=w_scales[r:P:32, :, :].bitcast(I32),
                 in_=Wf_scales[:, r:16:4, :].rearrange("g q n -> q g n").bitcast(I32),
             )
         load_weight_half(0)
-        for c in range(1, CHUNKS):
+        for c in range(2, CHUNKS):
             load_chunk(c)
         load_weight_half(1)
 
@@ -102,10 +103,10 @@ def tile_iag_pb_kernel(tc, T1, T2, Wf_words, Wf_scales, bn_g, bn_b, out):
         offset = gb_cols[:, O_TILES : 2 * O_TILES]
         stats = keep.tile([P, O_TILES, CHUNKS, BN_STATS_DIM], F32, name="stats")
         mean_var = keep.tile([P, O_TILES, 2], F32, name="mean_var")
-        std = keep.tile([P, O_TILES], F32, name="std")
+        neg_gain = keep.tile([P, O_TILES], F32, name="neg_gain")
+        neg_mean_gain = keep.tile([P, O_TILES], F32, name="neg_mean_gain")
         rstd = keep.tile([P, O_TILES], F32, name="rstd")
         scale = keep.tile([P, O_TILES], F32, name="scale")
-        mean_scaled = keep.tile([P, O_TILES], F32, name="mean_scaled")
         shift = keep.tile([P, O_TILES], F32, name="shift")
 
         def spread_gain_and_offset():
@@ -113,6 +114,7 @@ def tile_iag_pb_kernel(tc, T1, T2, Wf_words, Wf_scales, bn_g, bn_b, out):
             gb_t = bank(CHUNKS - 1)
             nc.tensor.transpose(gb_t[:, 0, 0:P], gb_wide[:], ident[:])
             nc.vector.tensor_copy(out=gb_cols[:], in_=gb_t[:, 0, 0 : 2 * O_TILES])
+            nc.vector.tensor_scalar_mul(out=neg_gain[:], in0=gain, scalar1=-1.0)
 
         x_codes = [
             keep.tile([P, STREAMS, CHUNK_ROWS], U32, name="x_codes%d" % c, align_bytes=64) for c in range(CHUNKS)
@@ -158,18 +160,22 @@ def tile_iag_pb_kernel(tc, T1, T2, Wf_words, Wf_scales, bn_g, bn_b, out):
             for jj in range(O_PER_HALF):
                 nc.vector.bn_stats(out=stats[:, h * O_PER_HALF + jj, c, :], in_=y[:, jj, :])
 
-        def deviation(h):
-            js = slice(h * O_PER_HALF, (h + 1) * O_PER_HALF)
-            for j in range(h * O_PER_HALF, (h + 1) * O_PER_HALF):
-                nc.vector.bn_aggr(out=mean_var[:, j, :], in_=stats[:, j, :, :].rearrange("p c s -> p (c s)"))
-            nc.scalar.activation(out=std[:, js], in_=mean_var[:, js, 1], func=ACT.Sqrt, bias=eps[:, 0:1])
-
         def scale_and_shift(h):
+            tiles = range(h * O_PER_HALF, (h + 1) * O_PER_HALF)
             js = slice(h * O_PER_HALF, (h + 1) * O_PER_HALF)
-            nc.vector.reciprocal(out=rstd[:, js], in_=std[:, js])
-            nc.vector.tensor_mul(out=scale[:, js], in0=rstd[:, js], in1=gain[:, js])
-            nc.vector.tensor_mul(out=mean_scaled[:, js], in0=mean_var[:, js, 0], in1=scale[:, js])
-            nc.vector.tensor_sub(out=shift[:, js], in0=offset[:, js], in1=mean_scaled[:, js])
+            for j in tiles:
+                nc.vector.bn_aggr(out=mean_var[:, j, :], in_=stats[:, j, :, :].rearrange("p c s -> p (c s)"))
+            nc.vector.tensor_mul(out=neg_mean_gain[:, js], in0=mean_var[:, js, 0], in1=neg_gain[:, js])
+            nc.scalar.activation(
+                out=rstd[:, js], in_=mean_var[:, js, 1], func=ACT.Abs_reciprocal_sqrt, bias=eps[:, 0:1]
+            )
+            for j in tiles:
+                one = slice(j, j + 1)
+                nc.scalar.activation(out=scale[:, one], in_=rstd[:, one], func=ACT.Identity, scale=gain[:, one])
+                nc.scalar.activation(
+                    out=shift[:, one], in_=rstd[:, one], func=ACT.Identity,
+                    scale=neg_mean_gain[:, one], bias=offset[:, one],
+                )
 
         def normalise(h, y):
             z = norm_pool.tile([P, O_PER_HALF, CHUNK_ROWS], F32, tag="z")
@@ -181,36 +187,34 @@ def tile_iag_pb_kernel(tc, T1, T2, Wf_words, Wf_scales, bn_g, bn_b, out):
                 )
             return z
 
-        def transpose_back_and_store(h, c, z, k, copy):
+        def transpose_back_and_store(h, c, z, k):
             z_t = bank(k)
             for i in range(TILES_PER_CHUNK):
                 for jj in range(O_PER_HALF):
                     nc.tensor.transpose(z_t[:, i, jj * P : (jj + 1) * P], z[:, jj, i * P : (i + 1) * P], ident[:])
             result = result_pool.tile([P, TILES_PER_CHUNK, HALF], F32, tag="result")
-            copy(out=result[:], in_=z_t[:])
+            nc.vector.tensor_copy(out=result[:], in_=z_t[:])
             nc.sync.dma_start(
                 out=out_rows[:, c * TILES_PER_CHUNK : (c + 1) * TILES_PER_CHUNK, h * HALF : (h + 1) * HALF],
                 in_=result[:],
             )
 
         y_first = []
-        for c in range(CHUNKS):
-            grouped = [transpose_in(c, g) for g in range(STREAMS)]
-            if c == 1:
-                spread_gain_and_offset()
-            for g in range(STREAMS):
-                quantise(c, g, grouped[g])
-            if c >= 1:
-                y_first.append(multiply(0, c - 1))
-                statistics(0, c - 1, y_first[c - 1])
-        y_first.append(multiply(0, CHUNKS - 1))
-        statistics(0, CHUNKS - 1, y_first[CHUNKS - 1])
+        for c in range(CHUNKS + LAG):
+            if c < CHUNKS:
+                grouped = [transpose_in(c, g) for g in range(STREAMS)]
+                if c == 1:
+                    spread_gain_and_offset()
+                for g in range(STREAMS):
+                    quantise(c, g, grouped[g])
+            if c >= LAG:
+                y_first.append(multiply(0, c - LAG))
+                statistics(0, c - LAG, y_first[c - LAG])
 
-        deviation(0)
-        y_second = [multiply(1, c) for c in range(BANKS - CHUNKS)]
-        statistics(1, 0, y_second[0])
         scale_and_shift(0)
-        for c in range(1, BANKS - CHUNKS):
+        y_second = []
+        for c in range(BANKS - CHUNKS):
+            y_second.append(multiply(1, c))
             statistics(1, c, y_second[c])
 
         z_first = []
@@ -220,12 +224,9 @@ def tile_iag_pb_kernel(tc, T1, T2, Wf_words, Wf_scales, bn_g, bn_b, out):
             if c_next < CHUNKS:
                 y_second.append(multiply(1, c_next))
                 statistics(1, c_next, y_second[c_next])
+        scale_and_shift(1)
         for c in range(CHUNKS):
-            copy = nc.scalar.copy if c < SCALAR_COPIES else nc.vector.tensor_copy
-            transpose_back_and_store(0, c, z_first[c], 2 * CHUNKS - BANKS + c % (BANKS - CHUNKS), copy)
-            if c == 0:
-                deviation(1)
-                scale_and_shift(1)
+            transpose_back_and_store(0, c, z_first[c], 2 * CHUNKS - BANKS + c % (BANKS - CHUNKS))
         for c in range(CHUNKS):
             z = normalise(1, y_second[c])
-            transpose_back_and_store(1, c, z, y_bank(1, c), nc.vector.tensor_copy)
+            transpose_back_and_store(1, c, z, y_bank(1, c))

@@ -28,6 +28,7 @@ BN_STATS_DIM = 6
 BANKS = 8
 HALF = O_PER_HALF * P
 LAG = 2
+IDLE_MATMULS = 4
 
 FLOPS = 2 * ROWS * STREAMS * EMB * EMB
 
@@ -50,6 +51,15 @@ def tile_iag_pb_kernel(tc, T1, T2, Wf_words, Wf_scales, bn_g, bn_b, out):
 
         def y_bank(h, c):
             return (h * CHUNKS + c) % BANKS
+
+        zeros = keep.tile([P, CHUNK_ROWS], F32, name="zeros")
+        nc.vector.memset(zeros[:], 0.0)
+        idle = bank(0)
+        for k in range(IDLE_MATMULS):
+            nc.tensor.matmul(
+                out=idle[:].rearrange("p a b -> p (a b)"), lhsT=zeros[:].bitcast(BF16)[:, 0:P], rhs=zeros[:].bitcast(BF16),
+                start=True, stop=True,
+            )
 
         gb_rows = keep.tile([2 * O_TILES, P], BF16, name="gb_rows")
         nc.scalar.dma_start(out=gb_rows[0:O_TILES, :], in_=bn_g.rearrange("(j o) -> j o", o=P))

@@ -10,6 +10,7 @@ U32 = mybir.dt.uint32
 U8 = mybir.dt.uint8
 FP8X4 = mybir.dt.float8_e4m3fn_x4
 ACT = mybir.ActivationFunctionType
+ALU = mybir.AluOpType
 
 P = 128
 ROWS = 1280
@@ -22,13 +23,15 @@ CHUNK_ROWS = TILES_PER_CHUNK * P
 O_TILES = EMB // P
 HALVES = 2
 O_PER_HALF = O_TILES // HALVES
+HALF = O_PER_HALF * P
 WORDS = EMB // 2
 BN_EPS = 1e-5
 BN_STATS_DIM = 6
-BANKS = 8
-HALF = O_PER_HALF * P
-LAG = 2
-IDLE_MATMULS = 4
+BANK = 512
+SPANS = ((0, 1), (1, 1), (2, 1), (3, 1), (4, 1))
+SPAN_OF = dict((c0 + k, (s, k)) for s, (c0, n) in enumerate(SPANS) for k in range(n))
+X_BANKS = (5, 6, 7)
+WARM = 4
 
 FLOPS = 2 * ROWS * STREAMS * EMB * EMB
 
@@ -40,30 +43,24 @@ def tile_iag_pb_kernel(tc, T1, T2, Wf_words, Wf_scales, bn_g, bn_b, out):
 
     with ExitStack() as ctx:
         keep = ctx.enter_context(tc.tile_pool(name="keep", bufs=1))
-        stage = ctx.enter_context(tc.tile_pool(name="stage", bufs=4))
-        norm_pool = ctx.enter_context(tc.tile_pool(name="norm", bufs=CHUNKS))
-        result_pool = ctx.enter_context(tc.tile_pool(name="result", bufs=HALVES * CHUNKS))
+        stage = ctx.enter_context(tc.tile_pool(name="stage", bufs=10))
         psum = ctx.enter_context(tc.psum_pool(name="psum", bufs=1))
         ctx.enter_context(tc.manual_schedule())
 
         def bank(k):
-            return psum.tile([P, 2, CHUNK_ROWS], F32, tag="bank%d" % k, name="bank%d" % k)
-
-        def y_bank(h, c):
-            return (h * CHUNKS + c) % BANKS
-
-        zeros = keep.tile([P, CHUNK_ROWS], F32, name="zeros")
-        nc.vector.memset(zeros[:], 0.0)
-        idle = bank(0)
-        for k in range(IDLE_MATMULS):
-            nc.tensor.matmul(
-                out=idle[:].rearrange("p a b -> p (a b)"), lhsT=zeros[:].bitcast(BF16)[:, 0:P], rhs=zeros[:].bitcast(BF16),
-                start=True, stop=True,
-            )
+            return psum.tile([P, BANK], F32, tag="bank%d" % k, name="bank%d" % k)
 
         gb_rows = keep.tile([2 * O_TILES, P], BF16, name="gb_rows")
         nc.scalar.dma_start(out=gb_rows[0:O_TILES, :], in_=bn_g.rearrange("(j o) -> j o", o=P))
         nc.scalar.dma_start(out=gb_rows[O_TILES : 2 * O_TILES, :], in_=bn_b.rearrange("(j o) -> j o", o=P))
+
+        if WARM:
+            zeros32 = keep.tile([P, BANK // 2], F32, name="zeros32")
+            nc.vector.memset(zeros32[:], 0.0)
+            zeros = zeros32[:].bitcast(BF16)
+            idle = bank(0)
+            for k in range(WARM):
+                nc.tensor.matmul(out=idle[:], lhsT=zeros[:, 0:P], rhs=zeros, start=True, stop=True)
 
         w_scales = keep.tile([P, STREAMS, EMB], U8, name="w_scales", align_bytes=64)
         nc.vector.memset(w_scales[:].rearrange("p g n -> p (g n)").bitcast(I32), 0)
@@ -111,7 +108,7 @@ def tile_iag_pb_kernel(tc, T1, T2, Wf_words, Wf_scales, bn_g, bn_b, out):
         gb_cols = keep.tile([P, 2 * O_TILES], F32, name="gb_cols")
         gain = gb_cols[:, 0:O_TILES]
         offset = gb_cols[:, O_TILES : 2 * O_TILES]
-        stats = keep.tile([P, O_TILES, CHUNKS, BN_STATS_DIM], F32, name="stats")
+        stats = keep.tile([P, O_TILES, len(SPANS), BN_STATS_DIM], F32, name="stats")
         mean_var = keep.tile([P, O_TILES, 2], F32, name="mean_var")
         neg_gain = keep.tile([P, O_TILES], F32, name="neg_gain")
         neg_mean_gain = keep.tile([P, O_TILES], F32, name="neg_mean_gain")
@@ -119,124 +116,205 @@ def tile_iag_pb_kernel(tc, T1, T2, Wf_words, Wf_scales, bn_g, bn_b, out):
         scale = keep.tile([P, O_TILES], F32, name="scale")
         shift = keep.tile([P, O_TILES], F32, name="shift")
 
-        def spread_gain_and_offset():
+        gb_bank = {}
+
+        def gb1():
             nc.vector.tensor_copy(out=gb_wide[0 : 2 * O_TILES, :], in_=gb_rows[:])
-            gb_t = bank(CHUNKS - 1)
-            nc.tensor.transpose(gb_t[:, 0, 0:P], gb_wide[:], ident[:])
-            nc.vector.tensor_copy(out=gb_cols[:], in_=gb_t[:, 0, 0 : 2 * O_TILES])
+
+        def gb2():
+            gb_bank[0] = bank(4)
+            nc.tensor.transpose(gb_bank[0][:, 0:P], gb_wide[:], ident[:])
+
+        def gb3():
+            nc.vector.tensor_copy(out=gb_cols[:], in_=gb_bank[0][:, 0 : 2 * O_TILES])
             nc.vector.tensor_scalar_mul(out=neg_gain[:], in0=gain, scalar1=-1.0)
 
         x_codes = [
-            keep.tile([P, STREAMS, CHUNK_ROWS], U32, name="x_codes%d" % c, align_bytes=64) for c in range(CHUNKS)
+            keep.tile([P, STREAMS, n * CHUNK_ROWS], U32, name="x_codes%d" % s, align_bytes=64)
+            for s, (c0, n) in enumerate(SPANS)
         ]
         x_scales = [
-            keep.tile([P, STREAMS, CHUNK_ROWS], U8, name="x_scales%d" % c, align_bytes=64) for c in range(CHUNKS)
+            keep.tile([P, STREAMS, n * CHUNK_ROWS], U8, name="x_scales%d" % s, align_bytes=64)
+            for s, (c0, n) in enumerate(SPANS)
         ]
 
-        def transpose_in(c, g):
-            x_t = bank(CHUNKS + (c * STREAMS + g) % (BANKS - CHUNKS))
+        x_ts = {}
+        grouped = {}
+
+        def T(c, g):
+            x_t = bank(X_BANKS[(c * STREAMS + g) % len(X_BANKS)])
+            halves = x_t[:].rearrange("p (u r) -> p u r", u=2)
             for i in range(TILES_PER_CHUNK):
                 words = x_chunks[c][:, g, i, :].bitcast(F32)
                 for u in range(2):
-                    nc.tensor.transpose(x_t[:, u, i * P : (i + 1) * P], words[:, u:WORDS:2], ident[:])
-            grouped = stage.tile([P, CHUNK_ROWS, 4], BF16, tag="grouped", align_bytes=64)
-            nc.scalar.copy(out=grouped[:].bitcast(F32), in_=x_t[:].rearrange("p u r -> p r u"))
-            return grouped
+                    nc.tensor.transpose(halves[:, u, i * P : (i + 1) * P], words[:, u:WORDS:2], ident[:])
+            x_ts[(c, g)] = halves
 
-        def quantise(c, g, grouped):
+        def a(c, g, engine="s"):
+            t = stage.tile([P, CHUNK_ROWS, 4], BF16, tag="grouped", align_bytes=64)
+            if engine == "s":
+                nc.scalar.copy(out=t[:].bitcast(F32), in_=x_ts[(c, g)].rearrange("p u r -> p r u"))
+            else:
+                nc.vector.tensor_copy(out=t[:].bitcast(F32), in_=x_ts[(c, g)].rearrange("p u r -> p r u"))
+            grouped[(c, g)] = t
+
+        def q(c, g):
+            s, k = SPAN_OF[c]
+            cols = slice(k * CHUNK_ROWS, (k + 1) * CHUNK_ROWS)
             nc.vector.quantize_mx(
-                out=x_codes[c][:, g, :].bitcast(FP8X4),
-                scales=x_scales[c][:, g, :],
-                in_=grouped[:].rearrange("p r t -> p (r t)"),
+                out=x_codes[s][:, g, cols].bitcast(FP8X4),
+                scales=x_scales[s][:, g, cols],
+                in_=grouped[(c, g)][:].rearrange("p r t -> p (r t)"),
             )
 
-        def multiply(h, c):
-            y = bank(y_bank(h, c))
-            for jj in range(O_PER_HALF):
-                j = h * O_PER_HALF + jj
-                for g in range(STREAMS):
-                    nc.tensor.matmul_mx(
-                        out=y[:, jj, :],
-                        lhsT=w_words[:, g, j * P : (j + 1) * P].bitcast(FP8X4),
-                        lhsT_scale=w_scales[:, g, j * P : (j + 1) * P],
-                        rhs=x_codes[c][:, g, :].bitcast(FP8X4),
-                        rhs_scale=x_scales[c][:, g, :],
-                        start=(g == 0),
-                        stop=(g == STREAMS - 1),
-                    )
-            return y
+        y_tiles = {}
 
-        def statistics(h, c, y):
-            for jj in range(O_PER_HALF):
-                nc.vector.bn_stats(out=stats[:, h * O_PER_HALF + jj, c, :], in_=y[:, jj, :])
-
-        def scale_and_shift(h):
-            tiles = range(h * O_PER_HALF, (h + 1) * O_PER_HALF)
-            js = slice(h * O_PER_HALF, (h + 1) * O_PER_HALF)
-            for j in tiles:
-                nc.vector.bn_aggr(out=mean_var[:, j, :], in_=stats[:, j, :, :].rearrange("p c s -> p (c s)"))
-            nc.vector.tensor_mul(out=neg_mean_gain[:, js], in0=mean_var[:, js, 0], in1=neg_gain[:, js])
-            nc.scalar.activation(
-                out=rstd[:, js], in_=mean_var[:, js, 1], func=ACT.Abs_reciprocal_sqrt, bias=eps[:, 0:1]
-            )
-            for j in tiles:
-                one = slice(j, j + 1)
-                nc.scalar.activation(out=scale[:, one], in_=rstd[:, one], func=ACT.Identity, scale=gain[:, one])
-                nc.scalar.activation(
-                    out=shift[:, one], in_=rstd[:, one], func=ACT.Identity,
-                    scale=neg_mean_gain[:, one], bias=offset[:, one],
+        def multiply(j, s, y, col0):
+            n = SPANS[s][1] * CHUNK_ROWS
+            for g in range(STREAMS):
+                nc.tensor.matmul_mx(
+                    out=y[:, col0 : col0 + n],
+                    lhsT=w_words[:, g, j * P : (j + 1) * P].bitcast(FP8X4),
+                    lhsT_scale=w_scales[:, g, j * P : (j + 1) * P],
+                    rhs=x_codes[s][:, g, :].bitcast(FP8X4),
+                    rhs_scale=x_scales[s][:, g, :],
+                    start=(g == 0),
+                    stop=(g == STREAMS - 1),
                 )
+            y_tiles[(j, s)] = y[:, col0 : col0 + n]
 
-        def normalise(h, y):
-            z = norm_pool.tile([P, O_PER_HALF, CHUNK_ROWS], F32, tag="z")
-            for jj in range(O_PER_HALF):
-                j = h * O_PER_HALF + jj
+        def statistics(j, s):
+            nc.vector.bn_stats(out=stats[:, j, s, :], in_=y_tiles[(j, s)])
+
+        def sv(j):
+            one = slice(j, j + 1)
+            nc.vector.bn_aggr(out=mean_var[:, j, :], in_=stats[:, j, :, :].rearrange("p c s -> p (c s)"))
+            nc.vector.tensor_mul(out=neg_mean_gain[:, one], in0=mean_var[:, one, 0], in1=neg_gain[:, one])
+
+        def sa(j):
+            one = slice(j, j + 1)
+            nc.scalar.activation(out=rstd[:, one], in_=mean_var[:, one, 1], func=ACT.Abs_reciprocal_sqrt, bias=eps[:, 0:1])
+            nc.scalar.activation(out=scale[:, one], in_=rstd[:, one], func=ACT.Identity, scale=gain[:, one])
+            nc.scalar.activation(
+                out=shift[:, one], in_=rstd[:, one], func=ACT.Identity,
+                scale=neg_mean_gain[:, one], bias=offset[:, one],
+            )
+
+        def scale_and_shift(j):
+            sv(j)
+            sa(j)
+
+        z_all = [keep.tile([P, ROWS], F32, name="z%d" % j) for j in range(O_TILES)]
+
+        y_sb = [keep.tile([P, CHUNKS, BANK], F32, name="y_sb%d" % h) for h in range(HALVES)]
+        moved = set()
+        y_banks = {}
+
+        def ev(h, c, engine="s"):
+            if engine == "s":
+                nc.scalar.copy(out=y_sb[h][:, c, :], in_=y_banks[(h, c)][:])
+            else:
+                nc.vector.tensor_copy(out=y_sb[h][:, c, :], in_=y_banks[(h, c)][:])
+            moved.add((2 * h, c))
+            moved.add((2 * h + 1, c))
+
+        def normalise(j, s, engine="s"):
+            r0 = SPANS[s][0] * CHUNK_ROWS
+            n_ = SPANS[s][1] * CHUNK_ROWS
+            jj = j % O_PER_HALF
+            src = y_sb[j // O_PER_HALF][:, s, jj * CHUNK_ROWS : (jj + 1) * CHUNK_ROWS] if (j, s) in moved else y_tiles[(j, s)]
+            if engine == "s":
                 nc.scalar.activation(
-                    out=z[:, jj, :], in_=y[:, jj, :], func=ACT.Relu,
+                    out=z_all[j][:, r0 : r0 + n_], in_=src, func=ACT.Identity,
                     bias=shift[:, j : j + 1], scale=scale[:, j : j + 1],
                 )
-            return z
+            else:
+                eng = nc.vector if engine == "v" else nc.gpsimd
+                eng.tensor_scalar(
+                    out=z_all[j][:, r0 : r0 + n_], in0=src, scalar1=scale[:, j : j + 1], scalar2=shift[:, j : j + 1],
+                    op0=ALU.mult, op1=ALU.add,
+                )
 
-        def transpose_back_and_store(h, c, z, k):
+        def nw(j, c0, k, engine="g"):
+            jj = j % O_PER_HALF
+            src = y_sb[j // O_PER_HALF][:, c0 : c0 + k, jj * CHUNK_ROWS : (jj + 1) * CHUNK_ROWS]
+            dst = z_all[j][:, c0 * CHUNK_ROWS : (c0 + k) * CHUNK_ROWS].rearrange("p (c r) -> p c r", c=k)
+            eng = {"g": nc.gpsimd, "v": nc.vector}[engine]
+            eng.tensor_scalar(
+                out=dst, in0=src, scalar1=scale[:, j : j + 1], scalar2=shift[:, j : j + 1], op0=ALU.mult, op1=ALU.add,
+            )
+
+        z_ts = {}
+
+        def transpose_back(h, c, k):
             z_t = bank(k)
             for i in range(TILES_PER_CHUNK):
                 for jj in range(O_PER_HALF):
-                    nc.tensor.transpose(z_t[:, i, jj * P : (jj + 1) * P], z[:, jj, i * P : (i + 1) * P], ident[:])
-            result = result_pool.tile([P, TILES_PER_CHUNK, HALF], F32, tag="result")
-            nc.vector.tensor_copy(out=result[:], in_=z_t[:])
+                    r0 = (c * TILES_PER_CHUNK + i) * P
+                    nc.tensor.transpose(
+                        z_t[:, (i * O_PER_HALF + jj) * P : (i * O_PER_HALF + jj + 1) * P],
+                        z_all[h * O_PER_HALF + jj][:, r0 : r0 + P], ident[:],
+                    )
+            z_ts[(h, c)] = z_t
+
+        def store(h, c, engine):
+            result = keep.tile([P, TILES_PER_CHUNK, HALF], F32, name="result%d_%d" % (h, c))
+            flat = result[:].rearrange("p i o -> p (i o)")
+            if engine == "v":
+                nc.vector.tensor_scalar_max(out=flat, in0=z_ts[(h, c)][:], scalar1=0.0)
+            else:
+                nc.scalar.activation(out=flat, in_=z_ts[(h, c)][:], func=ACT.Relu)
             nc.sync.dma_start(
                 out=out_rows[:, c * TILES_PER_CHUNK : (c + 1) * TILES_PER_CHUNK, h * HALF : (h + 1) * HALF],
                 in_=result[:],
             )
 
-        y_first = []
-        for c in range(CHUNKS + LAG):
-            if c < CHUNKS:
-                grouped = [transpose_in(c, g) for g in range(STREAMS)]
-                if c == 1:
-                    spread_gain_and_offset()
-                for g in range(STREAMS):
-                    quantise(c, g, grouped[g])
-            if c >= LAG:
-                y_first.append(multiply(0, c - LAG))
-                statistics(0, c - LAG, y_first[c - LAG])
+        M, st, ss, n, C, e = multiply, statistics, scale_and_shift, normalise, transpose_back, store
 
-        scale_and_shift(0)
-        y_second = []
-        for c in range(BANKS - CHUNKS):
-            y_second.append(multiply(1, c))
-            statistics(1, c, y_second[c])
-
-        z_first = []
-        for c in range(CHUNKS):
-            z_first.append(normalise(0, y_first[c]))
-            c_next = BANKS - CHUNKS + c
-            if c_next < CHUNKS:
-                y_second.append(multiply(1, c_next))
-                statistics(1, c_next, y_second[c_next])
-        scale_and_shift(1)
-        for c in range(CHUNKS):
-            transpose_back_and_store(0, c, z_first[c], 2 * CHUNKS - BANKS + c % (BANKS - CHUNKS))
-        for c in range(CHUNKS):
-            z = normalise(1, y_second[c])
-            transpose_back_and_store(1, c, z, y_bank(1, c))
+        def MM(h, c, k):
+            b = bank(k)
+            y_banks[(h, c)] = b
+            M(2 * h, c, b, 0)
+            M(2 * h + 1, c, b, CHUNK_ROWS)
+        def SS(h, c):
+            st(2 * h, c); st(2 * h + 1, c)
+        def NN(h, c, eng="s"):
+            n(2 * h, c, eng); n(2 * h + 1, c, eng)
+        def TA(c):
+            T(c, 0); a(c, 0); T(c, 1); a(c, 1)
+        def Q(c):
+            q(c, 0); q(c, 1)
+        gb1()
+        T(0, 0); gb2(); a(0, 0); T(0, 1); a(0, 1); gb3(); Q(0)
+        TA(1); Q(1)
+        TA(2); Q(2); MM(0, 0, 0); SS(0, 0)
+        TA(3); Q(3); MM(0, 1, 1); SS(0, 1)
+        TA(4); Q(4); MM(0, 2, 2); SS(0, 2)
+        ev(0, 0); ev(0, 1)
+        MM(0, 3, 3); SS(0, 3)
+        ev(0, 2)
+        MM(0, 4, 4); SS(0, 4)
+        ev(0, 3)
+        sv(0); sv(1); sa(0); sa(1)
+        MM(1, 0, 5); MM(1, 1, 6); MM(1, 2, 7); MM(1, 3, 0); MM(1, 4, 1)
+        nw(0, 0, 2); nw(1, 0, 2); nw(0, 2, 2); nw(1, 2, 2)
+        NN(0, 4); C(0, 4, 2)
+        SS(1, 0); SS(1, 1); SS(1, 2); SS(1, 3); SS(1, 4)
+        sv(2); sv(3)
+        C(0, 0, 3); C(0, 1, 4)
+        e(0, 4, "s");
+        e(0, 0, "s"); C(0, 2, 2)
+        e(0, 1, "s"); C(0, 3, 3)
+        sa(2); sa(3)
+        NN(1, 0, "v"); C(1, 0, 5)
+        e(0, 2, "s")
+        NN(1, 1, "v"); C(1, 1, 6)
+        e(0, 3, "s")
+        NN(1, 2, "v"); C(1, 2, 7)
+        NN(1, 3, "s"); C(1, 3, 0)
+        e(1, 0, "v")
+        NN(1, 4, "s"); C(1, 4, 1)
+        e(1, 1, "v")
+        e(1, 2, "s")
+        e(1, 3, "v")
+        e(1, 4, "s")

@@ -95,14 +95,15 @@ def tile_iag_pb_kernel(tc, T1, T2, Wf_words, Wf_scales, bn_g, bn_b, out):
 
         load_chunk(0)
         load_chunk(1)
+        load_chunk(2)
         for r in range(4):
             nc.sync.dma_start(
                 out=w_scales[r:P:32, :, :].bitcast(I32),
                 in_=Wf_scales[:, r:16:4, :].rearrange("g q n -> q g n").bitcast(I32),
             )
         load_weight_half(0)
-        for c in range(2, CHUNKS):
-            load_chunk(c)
+        load_chunk(3)
+        load_chunk(4)
         load_weight_half(1)
 
         gb_cols = keep.tile([P, 2 * O_TILES], F32, name="gb_cols")

@@ -305,8 +305,8 @@ def tile_iag_pb_kernel(tc, T1, T2, Wf_words, Wf_scales, bn_g, bn_b, out):
         C(0, 0, 3); C(0, 1, 4)
         e(0, 4, "s");
         e(0, 0, "s"); C(0, 2, 2)
-        e(0, 1, "s"); C(0, 3, 3)
         sa(2); sa(3)
+        e(0, 1, "s"); C(0, 3, 3)
         NN(1, 0, "v"); C(1, 0, 5)
         e(0, 2, "s")
         NN(1, 1, "v"); C(1, 1, 6)

@@ -79,6 +79,10 @@ def tile_iag_pb_kernel(tc, T1, T2, Wf_words, Wf_scales, bn_g, bn_b, out):
         def load_chunk(c):
             x_c = keep.tile([P, STREAMS, TILES_PER_CHUNK, EMB], BF16, name="x%d" % c)
             for g in range(STREAMS):
+                if c == 0 and g == 0:
+                    for i in range(TILES_PER_CHUNK):
+                        nc.sync.dma_start(out=x_c[:, g, i, :], in_=streams[g][:, i, :])
+                    continue
                 nc.sync.dma_start(
                     out=x_c[:, g, :, :],
                     in_=streams[g][:, c * TILES_PER_CHUNK : (c + 1) * TILES_PER_CHUNK, :],
@@ -94,13 +98,13 @@ def tile_iag_pb_kernel(tc, T1, T2, Wf_words, Wf_scales, bn_g, bn_b, out):
             )
 
         load_chunk(0)
-        load_chunk(1)
-        load_chunk(2)
         for r in range(4):
             nc.sync.dma_start(
                 out=w_scales[r:P:32, :, :].bitcast(I32),
                 in_=Wf_scales[:, r:16:4, :].rearrange("g q n -> q g n").bitcast(I32),
             )
+        load_chunk(1)
+        load_chunk(2)
         load_weight_half(0)
         load_chunk(3)
         load_chunk(4)
@@ -286,8 +290,8 @@ def tile_iag_pb_kernel(tc, T1, T2, Wf_words, Wf_scales, bn_g, bn_b, out):
         def Q(c):
             q(c, 0); q(c, 1)
         gb1()
-        T(0, 0); gb2(); a(0, 0); T(0, 1); a(0, 1); gb3(); Q(0)
-        TA(1); Q(1)
+        TA(0); Q(0)
+        T(1, 0); a(1, 0); T(1, 1); gb2(); a(1, 1); Q(1); gb3()
         TA(2); Q(2); MM(0, 0, 0); SS(0, 0)
         TA(3); Q(3); MM(0, 1, 1); SS(0, 1)
         TA(4); Q(4); MM(0, 2, 2); SS(0, 2)

@@ -98,12 +98,12 @@ def tile_iag_pb_kernel(tc, T1, T2, Wf_words, Wf_scales, bn_g, bn_b, out):
             )
 
         load_chunk(0)
+        load_chunk(1)
         for r in range(4):
             nc.sync.dma_start(
                 out=w_scales[r:P:32, :, :].bitcast(I32),
                 in_=Wf_scales[:, r:16:4, :].rearrange("g q n -> q g n").bitcast(I32),
             )
-        load_chunk(1)
         load_chunk(2)
         load_weight_half(0)
         load_chunk(3)

@@ -31,7 +31,7 @@ BANK = 512
 SPANS = ((0, 1), (1, 1), (2, 1), (3, 1), (4, 1))
 SPAN_OF = dict((c0 + k, (s, k)) for s, (c0, n) in enumerate(SPANS) for k in range(n))
 X_BANKS = (5, 6, 7)
-WARM = 4
+WARM = 3
 
 FLOPS = 2 * ROWS * STREAMS * EMB * EMB
 
@@ -172,6 +172,9 @@ def tile_iag_pb_kernel(tc, T1, T2, Wf_words, Wf_scales, bn_g, bn_b, out):
                 in_=grouped[(c, g)][:].rearrange("p r t -> p (r t)"),
             )
 
+        def keep_warm():
+            nc.tensor.matmul(out=idle[:], lhsT=zeros[:, 0:P], rhs=zeros, start=True, stop=True)
+
         y_tiles = {}
 
         def multiply(j, s, y, col0):
@@ -290,11 +293,11 @@ def tile_iag_pb_kernel(tc, T1, T2, Wf_words, Wf_scales, bn_g, bn_b, out):
         def Q(c):
             q(c, 0); q(c, 1)
         gb1()
-        TA(0); Q(0)
-        T(1, 0); a(1, 0); T(1, 1); gb2(); a(1, 1); Q(1); gb3()
-        TA(2); Q(2); MM(0, 0, 0); SS(0, 0)
-        TA(3); Q(3); MM(0, 1, 1); SS(0, 1)
-        TA(4); Q(4); MM(0, 2, 2); SS(0, 2)
+        T(0, 0); a(0, 0); T(0, 1); a(0, 1); keep_warm(); Q(0)
+        T(1, 0); a(1, 0); keep_warm(); T(1, 1); gb2(); a(1, 1); keep_warm(); Q(1); gb3()
+        T(2, 0); a(2, 0); keep_warm(); T(2, 1); a(2, 1); MM(0, 0, 0); q(2, 0); st(0, 0); q(2, 1); st(1, 0)
+        TA(3); MM(0, 1, 1); q(3, 0); st(0, 1); q(3, 1); st(1, 1)
+        TA(4); MM(0, 2, 2); q(4, 0); st(0, 2); q(4, 1); st(1, 2)
         ev(0, 0); ev(0, 1)
         MM(0, 3, 3); SS(0, 3)
         ev(0, 2)

@@ -194,23 +194,28 @@ def tile_iag_pb_kernel(tc, T1, T2, Wf_words, Wf_scales, bn_g, bn_b, out):
         def statistics(j, s):
             nc.vector.bn_stats(out=stats[:, j, s, :], in_=y_tiles[(j, s)])
 
-        def sv(j):
-            one = slice(j, j + 1)
-            nc.vector.bn_aggr(out=mean_var[:, j, :], in_=stats[:, j, :, :].rearrange("p c s -> p (c s)"))
-            nc.vector.tensor_mul(out=neg_mean_gain[:, one], in0=mean_var[:, one, 0], in1=neg_gain[:, one])
+        def sv(h):
+            pair = range(h * O_PER_HALF, (h + 1) * O_PER_HALF)
+            for j in pair:
+                nc.vector.bn_aggr(out=mean_var[:, j, :], in_=stats[:, j, :, :].rearrange("p c s -> p (c s)"))
+            for j in pair:
+                one = slice(j, j + 1)
+                nc.vector.tensor_mul(out=neg_mean_gain[:, one], in0=mean_var[:, one, 0], in1=neg_gain[:, one])
 
-        def sa(j):
-            one = slice(j, j + 1)
-            nc.scalar.activation(out=rstd[:, one], in_=mean_var[:, one, 1], func=ACT.Abs_reciprocal_sqrt, bias=eps[:, 0:1])
-            nc.scalar.activation(out=scale[:, one], in_=rstd[:, one], func=ACT.Identity, scale=gain[:, one])
-            nc.scalar.activation(
-                out=shift[:, one], in_=rstd[:, one], func=ACT.Identity,
-                scale=neg_mean_gain[:, one], bias=offset[:, one],
-            )
-
-        def scale_and_shift(j):
-            sv(j)
-            sa(j)
+        def sa(h):
+            pair = range(h * O_PER_HALF, (h + 1) * O_PER_HALF)
+            for j in pair:
+                one = slice(j, j + 1)
+                nc.scalar.activation(
+                    out=rstd[:, one], in_=mean_var[:, one, 1], func=ACT.Abs_reciprocal_sqrt, bias=eps[:, 0:1]
+                )
+            for j in pair:
+                one = slice(j, j + 1)
+                nc.scalar.activation(out=scale[:, one], in_=rstd[:, one], func=ACT.Identity, scale=gain[:, one])
+                nc.scalar.activation(
+                    out=shift[:, one], in_=rstd[:, one], func=ACT.Identity,
+                    scale=neg_mean_gain[:, one], bias=offset[:, one],
+                )
 
         z_all = [keep.tile([P, ROWS], F32, name="z%d" % j) for j in range(O_TILES)]
 
@@ -277,7 +282,7 @@ def tile_iag_pb_kernel(tc, T1, T2, Wf_words, Wf_scales, bn_g, bn_b, out):
                 in_=result[:],
             )
 
-        M, st, ss, n, C, e = multiply, statistics, scale_and_shift, normalise, transpose_back, store
+        M, st, n, C, e = multiply, statistics, normalise, transpose_back, store
 
         def MM(h, c, k):
             b = bank(k)
@@ -303,26 +308,26 @@ def tile_iag_pb_kernel(tc, T1, T2, Wf_words, Wf_scales, bn_g, bn_b, out):
         ev(0, 2)
         MM(0, 4, 4); SS(0, 4)
         ev(0, 3)
-        sv(0); sv(1); sa(0); sa(1)
+        sv(0); sa(0)
         MM(1, 0, 5); MM(1, 1, 6); MM(1, 2, 7); MM(1, 3, 0); MM(1, 4, 1)
         nw(0, 0, 2); nw(1, 0, 2); nw(0, 2, 2); nw(1, 2, 2)
         NN(0, 4); C(0, 4, 2)
         SS(1, 0); SS(1, 1); SS(1, 2); SS(1, 3); SS(1, 4)
-        sv(2); sv(3)
+        sv(1)
         C(0, 0, 3); C(0, 1, 4)
-        e(0, 4, "s");
+        e(0, 4, "s")
         e(0, 0, "s"); C(0, 2, 2)
-        sa(2); sa(3)
+        sa(1)
         e(0, 1, "s"); C(0, 3, 3)
         NN(1, 0, "v"); C(1, 0, 5)
         e(0, 2, "s")
         NN(1, 1, "v"); C(1, 1, 6)
         e(0, 3, "s")
         NN(1, 2, "v"); C(1, 2, 7)
-        NN(1, 3, "s"); C(1, 3, 0)
-        e(1, 0, "v")
-        NN(1, 4, "s"); C(1, 4, 1)
-        e(1, 1, "v")
-        e(1, 2, "s")
-        e(1, 3, "v")
-        e(1, 4, "s")
+        NN(1, 3, "v"); C(1, 3, 0)
+        e(1, 0, "s")
+        NN(1, 4, "v"); C(1, 4, 1)
+        e(1, 1, "s")
+        e(1, 2, "v")
+        e(1, 3, "s")
+        e(1, 4, "v")

@@ -307,22 +307,22 @@ def tile_iag_pb_kernel(tc, T1, T2, Wf_words, Wf_scales, bn_g, bn_b, out):
         MM(0, 3, 3); SS(0, 3)
         ev(0, 2)
         MM(0, 4, 4); SS(0, 4)
-        ev(0, 3)
         sv(0); sa(0)
         MM(1, 0, 5); MM(1, 1, 6); MM(1, 2, 7); MM(1, 3, 0); MM(1, 4, 1)
-        nw(0, 0, 2); nw(1, 0, 2); nw(0, 2, 2); nw(1, 2, 2)
+        nw(0, 0, 2); nw(1, 0, 2); nw(0, 2, 1); nw(1, 2, 1)
         NN(0, 4); C(0, 4, 2)
+        NN(0, 3); C(0, 3, 4)
         SS(1, 0); SS(1, 1); SS(1, 2); SS(1, 3); SS(1, 4)
         sv(1)
-        C(0, 0, 3); C(0, 1, 4)
         e(0, 4, "s")
-        e(0, 0, "s"); C(0, 2, 2)
+        C(0, 0, 3); C(0, 1, 2)
+        e(0, 3, "s"); C(0, 2, 4)
         sa(1)
-        e(0, 1, "s"); C(0, 3, 3)
+        e(0, 0, "s")
         NN(1, 0, "v"); C(1, 0, 5)
-        e(0, 2, "s")
+        e(0, 1, "s")
         NN(1, 1, "v"); C(1, 1, 6)
-        e(0, 3, "s")
+        e(0, 2, "s")
         NN(1, 2, "v"); C(1, 2, 7)
         NN(1, 3, "v"); C(1, 3, 0)
         e(1, 0, "s")

@@ -307,8 +307,9 @@ def tile_iag_pb_kernel(tc, T1, T2, Wf_words, Wf_scales, bn_g, bn_b, out):
         MM(0, 3, 3); SS(0, 3)
         ev(0, 2)
         MM(0, 4, 4); SS(0, 4)
+        MM(1, 0, 5); ev(1, 0)
         sv(0); sa(0)
-        MM(1, 0, 5); MM(1, 1, 6); MM(1, 2, 7); MM(1, 3, 0); MM(1, 4, 1)
+        MM(1, 1, 6); MM(1, 2, 7); MM(1, 3, 0); MM(1, 4, 1)
         nw(0, 0, 2); nw(1, 0, 2); nw(0, 2, 1); nw(1, 2, 1)
         NN(0, 4); C(0, 4, 2)
         NN(0, 3); C(0, 3, 4)

from contextlib import ExitStack

import concourse.mybir as mybir
from concourse.masks import make_identity

F32 = mybir.dt.float32
BF16 = mybir.dt.bfloat16
I32 = mybir.dt.int32
U32 = mybir.dt.uint32
U8 = mybir.dt.uint8
FP8X4 = mybir.dt.float8_e4m3fn_x4
ACT = mybir.ActivationFunctionType
ALU = mybir.AluOpType

P = 128
ROWS = 1280
EMB = 512
STREAMS = 2
ROW_TILES = ROWS // P
TILES_PER_CHUNK = 2
CHUNKS = ROW_TILES // TILES_PER_CHUNK
CHUNK_ROWS = TILES_PER_CHUNK * P
O_TILES = EMB // P
HALVES = 2
O_PER_HALF = O_TILES // HALVES
HALF = O_PER_HALF * P
WORDS = EMB // 2
BN_EPS = 1e-5
BN_STATS_DIM = 6
BANK = 512
SPANS = ((0, 1), (1, 1), (2, 1), (3, 1), (4, 1))
SPAN_OF = dict((c0 + k, (s, k)) for s, (c0, n) in enumerate(SPANS) for k in range(n))
X_BANKS = (5, 6, 7)
WARM = 3

FLOPS = 2 * ROWS * STREAMS * EMB * EMB


def tile_iag_pb_kernel(tc, T1, T2, Wf_words, Wf_scales, bn_g, bn_b, out):
    nc = tc.nc
    streams = [t.flatten_outer_dims().rearrange("(p i) c -> p i c", i=ROW_TILES) for t in (T1, T2)]
    out_rows = out.flatten_outer_dims().rearrange("(p i) o -> p i o", i=ROW_TILES)

    with ExitStack() as ctx:
        keep = ctx.enter_context(tc.tile_pool(name="keep", bufs=1))
        stage = ctx.enter_context(tc.tile_pool(name="stage", bufs=10))
        psum = ctx.enter_context(tc.psum_pool(name="psum", bufs=1))
        ctx.enter_context(tc.manual_schedule())

        def bank(k):
            return psum.tile([P, BANK], F32, tag="bank%d" % k, name="bank%d" % k)

        gb_rows = keep.tile([2 * O_TILES, P], BF16, name="gb_rows")
        nc.scalar.dma_start(out=gb_rows[0:O_TILES, :], in_=bn_g.rearrange("(j o) -> j o", o=P))
        nc.scalar.dma_start(out=gb_rows[O_TILES : 2 * O_TILES, :], in_=bn_b.rearrange("(j o) -> j o", o=P))

        if WARM:
            zeros32 = keep.tile([P, BANK // 2], F32, name="zeros32")
            nc.vector.memset(zeros32[:], 0.0)
            zeros = zeros32[:].bitcast(BF16)
            idle = bank(0)
            for k in range(WARM):
                nc.tensor.matmul(out=idle[:], lhsT=zeros[:, 0:P], rhs=zeros, start=True, stop=True)

        w_scales = keep.tile([P, STREAMS, EMB], U8, name="w_scales", align_bytes=64)
        nc.vector.memset(w_scales[:].rearrange("p g n -> p (g n)").bitcast(I32), 0)
        eps = keep.tile([P, 1], F32, name="eps")
        nc.vector.memset(eps[:], BN_EPS)
        warm = keep.tile([P, 1], F32, name="warm")
        nc.scalar.activation(out=warm[:], in_=eps[:], func=ACT.Abs_reciprocal_sqrt)
        gb_wide = keep.tile([P, P], F32, name="gb_wide")
        nc.vector.memset(gb_wide[:], 0.0)

        ident = keep.tile([P, P], F32, name="ident")
        make_identity(nc, ident[:])

        x_chunks = []

        def load_chunk(c):
            x_c = keep.tile([P, STREAMS, TILES_PER_CHUNK, EMB], BF16, name="x%d" % c)
            for g in range(STREAMS):
                if c == 0 and g == 0:
                    for i in range(TILES_PER_CHUNK):
                        nc.sync.dma_start(out=x_c[:, g, i, :], in_=streams[g][:, i, :])
                    continue
                nc.sync.dma_start(
                    out=x_c[:, g, :, :],
                    in_=streams[g][:, c * TILES_PER_CHUNK : (c + 1) * TILES_PER_CHUNK, :],
                )
            x_chunks.append(x_c)

        w_words = keep.tile([P, STREAMS, EMB], U32, name="w_words", align_bytes=64)

        def load_weight_half(h):
            nc.sync.dma_start(
                out=w_words[:, :, h * HALF : (h + 1) * HALF].bitcast(I32),
                in_=Wf_words[:, :, h * HALF : (h + 1) * HALF, :].rearrange("g p n t -> p g (n t)").bitcast(I32),
            )

        load_chunk(0)
        load_chunk(1)
        for r in range(4):
            nc.sync.dma_start(
                out=w_scales[r:P:32, :, :].bitcast(I32),
                in_=Wf_scales[:, r:16:4, :].rearrange("g q n -> q g n").bitcast(I32),
            )
        load_chunk(2)
        load_weight_half(0)
        load_chunk(3)
        load_chunk(4)
        load_weight_half(1)

        gb_cols = keep.tile([P, 2 * O_TILES], F32, name="gb_cols")
        gain = gb_cols[:, 0:O_TILES]
        offset = gb_cols[:, O_TILES : 2 * O_TILES]
        stats = keep.tile([P, O_TILES, len(SPANS), BN_STATS_DIM], F32, name="stats")
        mean_var = keep.tile([P, O_TILES, 2], F32, name="mean_var")
        neg_gain = keep.tile([P, O_TILES], F32, name="neg_gain")
        neg_mean_gain = keep.tile([P, O_TILES], F32, name="neg_mean_gain")
        rstd = keep.tile([P, O_TILES], F32, name="rstd")
        scale = keep.tile([P, O_TILES], F32, name="scale")
        shift = keep.tile([P, O_TILES], F32, name="shift")

        gb_bank = {}

        def gb1():
            nc.vector.tensor_copy(out=gb_wide[0 : 2 * O_TILES, :], in_=gb_rows[:])

        def gb2():
            gb_bank[0] = bank(4)
            nc.tensor.transpose(gb_bank[0][:, 0:P], gb_wide[:], ident[:])

        def gb3():
            nc.vector.tensor_copy(out=gb_cols[:], in_=gb_bank[0][:, 0 : 2 * O_TILES])
            nc.vector.tensor_scalar_mul(out=neg_gain[:], in0=gain, scalar1=-1.0)

        x_codes = [
            keep.tile([P, STREAMS, n * CHUNK_ROWS], U32, name="x_codes%d" % s, align_bytes=64)
            for s, (c0, n) in enumerate(SPANS)
        ]
        x_scales = [
            keep.tile([P, STREAMS, n * CHUNK_ROWS], U8, name="x_scales%d" % s, align_bytes=64)
            for s, (c0, n) in enumerate(SPANS)
        ]

        x_ts = {}
        grouped = {}

        def T(c, g):
            x_t = bank(X_BANKS[(c * STREAMS + g) % len(X_BANKS)])
            halves = x_t[:].rearrange("p (u r) -> p u r", u=2)
            for i in range(TILES_PER_CHUNK):
                words = x_chunks[c][:, g, i, :].bitcast(F32)
                for u in range(2):
                    nc.tensor.transpose(halves[:, u, i * P : (i + 1) * P], words[:, u:WORDS:2], ident[:])
            x_ts[(c, g)] = halves

        def a(c, g, engine="s"):
            t = stage.tile([P, CHUNK_ROWS, 4], BF16, tag="grouped", align_bytes=64)
            if engine == "s":
                nc.scalar.copy(out=t[:].bitcast(F32), in_=x_ts[(c, g)].rearrange("p u r -> p r u"))
            else:
                nc.vector.tensor_copy(out=t[:].bitcast(F32), in_=x_ts[(c, g)].rearrange("p u r -> p r u"))
            grouped[(c, g)] = t

        def q(c, g):
            s, k = SPAN_OF[c]
            cols = slice(k * CHUNK_ROWS, (k + 1) * CHUNK_ROWS)
            nc.vector.quantize_mx(
                out=x_codes[s][:, g, cols].bitcast(FP8X4),
                scales=x_scales[s][:, g, cols],
                in_=grouped[(c, g)][:].rearrange("p r t -> p (r t)"),
            )

        def keep_warm():
            nc.tensor.matmul(out=idle[:], lhsT=zeros[:, 0:P], rhs=zeros, start=True, stop=True)

        y_tiles = {}

        def multiply(j, s, y, col0):
            n = SPANS[s][1] * CHUNK_ROWS
            for g in range(STREAMS):
                nc.tensor.matmul_mx(
                    out=y[:, col0 : col0 + n],
                    lhsT=w_words[:, g, j * P : (j + 1) * P].bitcast(FP8X4),
                    lhsT_scale=w_scales[:, g, j * P : (j + 1) * P],
                    rhs=x_codes[s][:, g, :].bitcast(FP8X4),
                    rhs_scale=x_scales[s][:, g, :],
                    start=(g == 0),
                    stop=(g == STREAMS - 1),
                )
            y_tiles[(j, s)] = y[:, col0 : col0 + n]

        def statistics(j, s):
            nc.vector.bn_stats(out=stats[:, j, s, :], in_=y_tiles[(j, s)])

        def sv(h):
            pair = range(h * O_PER_HALF, (h + 1) * O_PER_HALF)
            for j in pair:
                nc.vector.bn_aggr(out=mean_var[:, j, :], in_=stats[:, j, :, :].rearrange("p c s -> p (c s)"))
            for j in pair:
                one = slice(j, j + 1)
                nc.vector.tensor_mul(out=neg_mean_gain[:, one], in0=mean_var[:, one, 0], in1=neg_gain[:, one])

        def sa(h):
            pair = range(h * O_PER_HALF, (h + 1) * O_PER_HALF)
            for j in pair:
                one = slice(j, j + 1)
                nc.scalar.activation(
                    out=rstd[:, one], in_=mean_var[:, one, 1], func=ACT.Abs_reciprocal_sqrt, bias=eps[:, 0:1]
                )
            for j in pair:
                one = slice(j, j + 1)
                nc.scalar.activation(out=scale[:, one], in_=rstd[:, one], func=ACT.Identity, scale=gain[:, one])
                nc.scalar.activation(
                    out=shift[:, one], in_=rstd[:, one], func=ACT.Identity,
                    scale=neg_mean_gain[:, one], bias=offset[:, one],
                )

        z_all = [keep.tile([P, ROWS], F32, name="z%d" % j) for j in range(O_TILES)]

        y_sb = [keep.tile([P, CHUNKS, BANK], F32, name="y_sb%d" % h) for h in range(HALVES)]
        moved = set()
        y_banks = {}

        def ev(h, c, engine="s"):
            if engine == "s":
                nc.scalar.copy(out=y_sb[h][:, c, :], in_=y_banks[(h, c)][:])
            else:
                nc.vector.tensor_copy(out=y_sb[h][:, c, :], in_=y_banks[(h, c)][:])
            moved.add((2 * h, c))
            moved.add((2 * h + 1, c))

        def normalise(j, s, engine="s"):
            r0 = SPANS[s][0] * CHUNK_ROWS
            n_ = SPANS[s][1] * CHUNK_ROWS
            jj = j % O_PER_HALF
            src = y_sb[j // O_PER_HALF][:, s, jj * CHUNK_ROWS : (jj + 1) * CHUNK_ROWS] if (j, s) in moved else y_tiles[(j, s)]
            if engine == "s":
                nc.scalar.activation(
                    out=z_all[j][:, r0 : r0 + n_], in_=src, func=ACT.Identity,
                    bias=shift[:, j : j + 1], scale=scale[:, j : j + 1],
                )
            else:
                eng = nc.vector if engine == "v" else nc.gpsimd
                eng.tensor_scalar(
                    out=z_all[j][:, r0 : r0 + n_], in0=src, scalar1=scale[:, j : j + 1], scalar2=shift[:, j : j + 1],
                    op0=ALU.mult, op1=ALU.add,
                )

        def nw(j, c0, k, engine="g"):
            jj = j % O_PER_HALF
            src = y_sb[j // O_PER_HALF][:, c0 : c0 + k, jj * CHUNK_ROWS : (jj + 1) * CHUNK_ROWS]
            dst = z_all[j][:, c0 * CHUNK_ROWS : (c0 + k) * CHUNK_ROWS].rearrange("p (c r) -> p c r", c=k)
            eng = {"g": nc.gpsimd, "v": nc.vector}[engine]
            eng.tensor_scalar(
                out=dst, in0=src, scalar1=scale[:, j : j + 1], scalar2=shift[:, j : j + 1], op0=ALU.mult, op1=ALU.add,
            )

        z_ts = {}

        def transpose_back(h, c, k):
            z_t = bank(k)
            for i in range(TILES_PER_CHUNK):
                for jj in range(O_PER_HALF):
                    r0 = (c * TILES_PER_CHUNK + i) * P
                    nc.tensor.transpose(
                        z_t[:, (i * O_PER_HALF + jj) * P : (i * O_PER_HALF + jj + 1) * P],
                        z_all[h * O_PER_HALF + jj][:, r0 : r0 + P], ident[:],
                    )
            z_ts[(h, c)] = z_t

        def store(h, c, engine):
            result = keep.tile([P, TILES_PER_CHUNK, HALF], F32, name="result%d_%d" % (h, c))
            flat = result[:].rearrange("p i o -> p (i o)")
            if engine == "v":
                nc.vector.tensor_scalar_max(out=flat, in0=z_ts[(h, c)][:], scalar1=0.0)
            else:
                nc.scalar.activation(out=flat, in_=z_ts[(h, c)][:], func=ACT.Relu)
            nc.sync.dma_start(
                out=out_rows[:, c * TILES_PER_CHUNK : (c + 1) * TILES_PER_CHUNK, h * HALF : (h + 1) * HALF],
                in_=result[:],
            )

        M, st, n, C, e = multiply, statistics, normalise, transpose_back, store

        def MM(h, c, k):
            b = bank(k)
            y_banks[(h, c)] = b
            M(2 * h, c, b, 0)
            M(2 * h + 1, c, b, CHUNK_ROWS)
        def SS(h, c):
            st(2 * h, c); st(2 * h + 1, c)
        def NN(h, c, eng="s"):
            n(2 * h, c, eng); n(2 * h + 1, c, eng)
        def TA(c):
            T(c, 0); a(c, 0); T(c, 1); a(c, 1)
        def Q(c):
            q(c, 0); q(c, 1)
        gb1()
        T(0, 0); a(0, 0); T(0, 1); a(0, 1); keep_warm(); Q(0)
        T(1, 0); a(1, 0); keep_warm(); T(1, 1); gb2(); a(1, 1); keep_warm(); Q(1); gb3()
        T(2, 0); a(2, 0); keep_warm(); T(2, 1); a(2, 1); MM(0, 0, 0); q(2, 0); st(0, 0); q(2, 1); st(1, 0)
        TA(3); MM(0, 1, 1); q(3, 0); st(0, 1); q(3, 1); st(1, 1)
        TA(4); MM(0, 2, 2); q(4, 0); st(0, 2); q(4, 1); st(1, 2)
        ev(0, 0); ev(0, 1)
        MM(0, 3, 3); SS(0, 3)
        ev(0, 2)
        MM(0, 4, 4); SS(0, 4)
        MM(1, 0, 5); ev(1, 0)
        sv(0); sa(0)
        MM(1, 1, 6); MM(1, 2, 7); MM(1, 3, 0); MM(1, 4, 1)
        nw(0, 0, 2); nw(1, 0, 2); nw(0, 2, 1); nw(1, 2, 1)
        NN(0, 4); C(0, 4, 2)
        NN(0, 3); C(0, 3, 4)
        SS(1, 0); SS(1, 1); SS(1, 2); SS(1, 3); SS(1, 4)
        sv(1)
        e(0, 4, "s")
        C(0, 0, 3); C(0, 1, 2)
        e(0, 3, "s"); C(0, 2, 4)
        sa(1)
        e(0, 0, "s")
        NN(1, 0, "v"); C(1, 0, 5)
        e(0, 1, "s")
        NN(1, 1, "v"); C(1, 1, 6)
        e(0, 2, "s")
        NN(1, 2, "v"); C(1, 2, 7)
        NN(1, 3, "v"); C(1, 3, 0)
        e(1, 0, "s")
        NN(1, 4, "v"); C(1, 4, 1)
        e(1, 1, "s")
        e(1, 2, "v")
        e(1, 3, "s")
        e(1, 4, "v")
